import numpy as np
import ml_dtypes


def mxq(x, axis, fmt="e4m3"):
    dtype, down = {"e4m3": (ml_dtypes.float8_e4m3fn, 7), "e5m2": (ml_dtypes.float8_e5m2, 14)}[fmt]
    v = np.moveaxis(np.asarray(x, np.float32).astype(ml_dtypes.bfloat16).astype(np.float64), axis, -1)
    blocks = v.reshape(v.shape[:-1] + (-1, 32))
    amax = np.abs(blocks).max(-1, keepdims=True)
    byte = np.maximum(np.where(amax > 0, np.frexp(amax)[1] - 1 + 127, 0) - down, 1)
    scale = np.exp2(byte - 127.0)
    codes = (blocks / scale).astype(np.float32).astype(dtype).astype(np.float64)
    return np.moveaxis((codes * scale).reshape(v.shape), -1, axis)


WIDE = False


def mx_kscale(k):
    if not WIDE:
        return np.ones(k)
    levels = np.array([10, -10, 5, -5, 0])
    a = np.random.permutation(np.resize(levels, k // 512 * 4)).reshape(k // 512, 4)
    idx = np.arange(k)
    return np.exp2(a[idx // 512, idx % 128 // 32])


BF16 = ml_dtypes.bfloat16


def bf(x):
    return np.asarray(x, np.float32).astype(BF16)


def f64(x):
    return np.asarray(x).astype(np.float64)


E2M1 = np.array([0.0, 0.5, 1.0, 1.5, 2.0, 3.0, 4.0, 6.0, -0.0, -0.5, -1.0, -1.5, -2.0, -3.0, -4.0, -6.0])


def pack_weight(w, fmt):
    k, n = w.shape
    w = f64(bf(w)).reshape(k // 32, 32, n)
    amax = np.abs(w).max(1)
    if fmt == "e4m3":
        byte = np.frexp(amax)[1] - 1 + 127 - 7
    else:
        mant, ex = np.frexp(amax / 6.0)
        byte = np.where(mant > 0.5, ex, ex - 1) + 127
    byte = np.clip(np.where(amax > 0, byte, 1), 1, 254)
    scaled = (w * np.exp2(127.0 - byte)[:, None, :]).reshape(k, n).astype(np.float32)
    by_word = np.ascontiguousarray(scaled.reshape(k // 512, 128, 4, n).transpose(0, 1, 3, 2))
    if fmt == "e4m3":
        words = by_word.astype(ml_dtypes.float8_e4m3fn).view(np.uint8)
    else:
        c = by_word.astype(ml_dtypes.float4_e2m1fn).view(np.uint8) & 0xF
        words = c[..., 0::2] | (c[..., 1::2] << 4)
    return np.ascontiguousarray(words), np.ascontiguousarray(byte.astype(np.uint8).reshape(k // 512, 16, n))


def unpack_weight(words, scales, fmt):
    g, p, n, _ = words.shape
    if fmt == "e4m3":
        vals = np.ascontiguousarray(words).view(ml_dtypes.float8_e4m3fn).astype(np.float64)
    else:
        nib = np.empty((g, p, n, 4), np.uint8)
        nib[..., 0::2] = words & 0xF
        nib[..., 1::2] = words >> 4
        vals = E2M1[nib]
    vals = vals * np.repeat(np.exp2(scales.astype(np.float64) - 127.0), 8, axis=1)[..., None]
    return vals.transpose(0, 1, 3, 2).reshape(g * 512, n)

def pack4(w):
    words, scales = pack_weight(w, "e2m1")
    return words.reshape(words.shape[0], 128, -1), scales


def unpack4(words, scales):
    return unpack_weight(words.reshape(words.shape[0], 128, -1, 2), scales, "e2m1")


B, K, D, H1, H2, C = 32, 4, 16384, 512, 512, 64
N = B * K


def setup_inputs():
    s = mx_kscale(D)
    nf1 = bf(np.random.standard_normal((N, D)) * s)
    nf2 = bf(np.random.standard_normal((N * K, D)) * s)
    w1_0_words, w1_0_scales = pack4(np.random.standard_normal((D, H1)) / np.sqrt(D) / s[:, None])
    w2_0_words, w2_0_scales = pack4(np.random.standard_normal((D, H1)) / np.sqrt(D) / s[:, None])
    return {"nf1": nf1,
            "nf2": nf2,
            "w1_0_words": w1_0_words,
            "w1_0_scales": w1_0_scales,
            "w2_0_words": w2_0_words,
            "w2_0_scales": w2_0_scales}


def sage_gcn(cur, neigh, w1, w2):
    b, d = cur.shape
    agg = neigh.reshape(b, -1, d).mean(axis=1)
    return np.maximum((mxq(cur, 1, "e4m3") @ w2) + (mxq(agg, 1, "e4m3") @ w1), 0.0)


def reference(nf1, nf2, w1_0_words, w1_0_scales, w2_0_words, w2_0_scales):
    return sage_gcn(f64(nf1), f64(nf2), unpack4(w1_0_words, w1_0_scales), unpack4(w2_0_words, w2_0_scales))

@@ -1,0 +1,187 @@
+from contextlib import ExitStack
+
+import concourse.mybir as mybir
+from concourse.masks import make_identity
+
+F32 = mybir.dt.float32
+BF16 = mybir.dt.bfloat16
+I32 = mybir.dt.int32
+U32 = mybir.dt.uint32
+U8 = mybir.dt.uint8
+FP8X4 = mybir.dt.float8_e4m3fn_x4
+FP4X4 = mybir.dt.float4_e2m1fn_x4
+ADD = mybir.AluOpType.add
+COPY = mybir.ActivationFunctionType.Copy
+RELU = mybir.ActivationFunctionType.Relu
+
+P = 128
+NEIGHBOURS = 4
+D = 16384
+H = 512
+PACK = 4
+K_PASS = P * PACK
+GROUPS = D // K_PASS
+CHUNK_GROUPS = 4
+CHUNK = CHUNK_GROUPS * K_PASS
+N_CHUNKS = GROUPS // CHUNK_GROUPS
+BANK_GROUPS = 2
+WORDS = K_PASS // 2
+LEAD = 2
+
+FLOPS = 2 * 2 * P * D * H
+
+
+def tile_graphsage_pa_k_kernel(
+    tc, nf1, nf2, w1_0_words, w1_0_scales, w2_0_words, w2_0_scales, out
+):
+    nc = tc.nc
+    weight_words = (w2_0_words.bitcast(I32), w1_0_words.bitcast(I32))
+    weight_scales = (w2_0_scales.bitcast(I32), w1_0_scales.bitcast(I32))
+    nf2_by_node = nf2.rearrange("(i j) d -> i j d", j=NEIGHBOURS)
+
+    with ExitStack() as ctx:
+        ctx.enter_context(tc.manual_schedule())
+        const = ctx.enter_context(tc.tile_pool(name="const", bufs=1))
+        features = ctx.enter_context(tc.tile_pool(name="features", bufs=LEAD + 2))
+        partial = ctx.enter_context(tc.tile_pool(name="partial", bufs=2))
+        summed = ctx.enter_context(tc.tile_pool(name="summed", bufs=3))
+        regrouped = ctx.enter_context(tc.tile_pool(name="regrouped", bufs=2))
+        quantised = ctx.enter_context(tc.tile_pool(name="quantised", bufs=LEAD + 2))
+        weights = ctx.enter_context(tc.tile_pool(name="weights", bufs=3))
+        flipped = ctx.enter_context(tc.psum_pool(name="flipped", bufs=4))
+        product = ctx.enter_context(tc.psum_pool(name="product", bufs=1))
+
+        identity = const.tile([P, P], F32)
+        make_identity(nc, identity[:])
+
+        w_planes = const.tile([P, 2, GROUPS, H], U8, align_bytes=64)
+        nc.vector.memset(w_planes[:].bitcast(I32), 0)
+
+        acc = product.tile([P, H], F32)
+
+        neighbour_rows = {}
+        own_rows = {}
+        sum_rows = {}
+        codes = {}
+        planes = {}
+        words = {}
+
+        def load_features(c):
+            cols = slice(c * CHUNK, (c + 1) * CHUNK)
+            neighbour_t = features.tile([P, NEIGHBOURS, CHUNK], BF16, tag="neighbour")
+            nc.sync.dma_start(out=neighbour_t[:], in_=nf2_by_node[:, :, cols])
+            own_t = features.tile([P, CHUNK], BF16, tag="own")
+            nc.sync.dma_start(out=own_t[:], in_=nf1[:, cols])
+            neighbour_rows[c] = neighbour_t
+            own_rows[c] = own_t
+
+        def load_weight_scales():
+            for a in range(2):
+                by_row = weight_scales[a].rearrange("g (h s) n -> s h g n", h=2)
+                for s in range(8):
+                    first = 32 * (s // 4) + s % 4
+                    nc.sync.dma_start(
+                        out=w_planes[first:P:64, a, :, :].bitcast(I32), in_=by_row[s]
+                    )
+
+        def load_weight_words(c):
+            for a in range(2):
+                words_t = weights.tile([P, CHUNK_GROUPS, 2 * H], U8, tag="words%d" % a, align_bytes=64)
+                nc.sync.dma_start(
+                    out=words_t[:].bitcast(I32),
+                    in_=weight_words[a][c * CHUNK_GROUPS : (c + 1) * CHUNK_GROUPS].rearrange(
+                        "g p n -> p g n"
+                    ),
+                )
+                words[(a, c)] = words_t
+
+        def add_first_pairs(c):
+            rows = neighbour_rows[c]
+            pair01 = partial.tile([P, CHUNK], F32, tag="pair01")
+            nc.vector.tensor_tensor(out=pair01[:], in0=rows[:, 0, :], in1=rows[:, 1, :], op=ADD)
+            pair23 = partial.tile([P, CHUNK], F32, tag="pair23")
+            nc.vector.tensor_tensor(out=pair23[:], in0=rows[:, 2, :], in1=rows[:, 3, :], op=ADD)
+            return pair01, pair23
+
+        def add_pairs(c, pair01, pair23):
+            sum_t = summed.tile([P, CHUNK], BF16, tag="sum")
+            nc.vector.tensor_tensor(out=sum_t[:], in0=pair01[:], in1=pair23[:], op=ADD)
+            sum_rows[c] = sum_t
+
+        def transpose_and_regroup(c):
+            grouped = []
+            for a, rows in enumerate((own_rows[c], sum_rows[c])):
+                row_words = rows[:].bitcast(F32)
+                grouped_t = regrouped.tile([P, CHUNK], BF16, tag="grouped%d" % a, align_bytes=64)
+                for b in range(CHUNK_GROUPS // BANK_GROUPS):
+                    bank = flipped.tile([P, 2, BANK_GROUPS, P], F32, tag="bank")
+                    for g in range(BANK_GROUPS):
+                        first = (b * BANK_GROUPS + g) * WORDS
+                        for u in range(2):
+                            nc.tensor.transpose(
+                                out=bank[:, u, g, :],
+                                in_=row_words[:, first + u : first + WORDS : 2],
+                                identity=identity[:],
+                            )
+                    nodes = slice(b * BANK_GROUPS * P, (b + 1) * BANK_GROUPS * P)
+                    if a == 0:
+                        nc.scalar.copy(
+                            out=grouped_t[:].bitcast(F32).rearrange("p (c u) -> p c u", u=2)[:, nodes, :],
+                            in_=bank[:].rearrange("p u g i -> p (g i) u"),
+                        )
+                    else:
+                        nc.scalar.activation(
+                            out=grouped_t[:].rearrange("p (c u e) -> p c u e", u=2, e=2)[:, nodes, :, :],
+                            in_=bank[:].bitcast(BF16).rearrange("p u g (i e) -> p (g i) u e", e=2),
+                            func=COPY,
+                            scale=1.0 / NEIGHBOURS,
+                        )
+                grouped.append(grouped_t)
+            return grouped
+
+        def quantise(c, grouped):
+            for a in range(2):
+                codes_t = quantised.tile([P, CHUNK_GROUPS * P], U32, tag="codes%d" % a, align_bytes=64)
+                plane_t = quantised.tile([P, CHUNK_GROUPS * P], U8, tag="plane%d" % a, align_bytes=64)
+                nc.vector.quantize_mx(
+                    out=codes_t[:].bitcast(FP8X4), scales=plane_t[:], in_=grouped[a][:]
+                )
+                codes[(a, c)] = codes_t
+                planes[(a, c)] = plane_t
+
+        def multiply(c):
+            for a in range(2):
+                for g in range(CHUNK_GROUPS):
+                    nodes = slice(g * P, (g + 1) * P)
+                    nc.tensor.matmul_mx(
+                        out=acc[:],
+                        lhsT=codes[(a, c)][:, nodes].bitcast(FP8X4),
+                        lhsT_scale=planes[(a, c)][:, nodes],
+                        rhs=words[(a, c)][:, g, :].bitcast(FP4X4),
+                        rhs_scale=w_planes[:, a, c * CHUNK_GROUPS + g, :],
+                        start=(c == 0 and a == 0 and g == 0),
+                        stop=(c == N_CHUNKS - 1 and a == 1 and g == CHUNK_GROUPS - 1),
+                    )
+
+        grouped_of = {}
+        for s in range(N_CHUNKS + LEAD):
+            if s < N_CHUNKS:
+                load_features(s)
+            if s == LEAD:
+                load_weight_scales()
+            if s >= LEAD:
+                load_weight_words(s - LEAD)
+            if s < N_CHUNKS:
+                pair01, pair23 = add_first_pairs(s)
+            if 1 <= s <= N_CHUNKS:
+                quantise(s - 1, grouped_of[s - 1])
+            if s < N_CHUNKS:
+                add_pairs(s, pair01, pair23)
+            if s >= LEAD:
+                multiply(s - LEAD)
+            if s < N_CHUNKS:
+                grouped_of[s] = transpose_and_regroup(s)
+
+        result = const.tile([P, H], F32)
+        nc.scalar.activation(out=result[:], in_=acc[:], func=RELU)
+        nc.sync.dma_start(out=out, in_=result[:])

@@ -26,7 +26,11 @@ CHUNK = CHUNK_GROUPS * K_PASS
 N_CHUNKS = GROUPS // CHUNK_GROUPS
 BANK_GROUPS = 2
 WORDS = K_PASS // 2
-LEAD = 2
+OWN = 0
+AGG = 1
+SCALE_ROWS = K_PASS // 32
+QUADRANTS = 4
+LAG = SCALE_ROWS // QUADRANTS
 
 FLOPS = 2 * 2 * P * D * H
 
@@ -42,14 +46,17 @@ def tile_graphsage_pa_k_kernel(
     with ExitStack() as ctx:
         ctx.enter_context(tc.manual_schedule())
         const = ctx.enter_context(tc.tile_pool(name="const", bufs=1))
-        features = ctx.enter_context(tc.tile_pool(name="features", bufs=LEAD + 2))
+        neighbours = ctx.enter_context(tc.tile_pool(name="neighbours", bufs=4))
+        own_features = ctx.enter_context(tc.tile_pool(name="own_features", bufs=3))
         partial = ctx.enter_context(tc.tile_pool(name="partial", bufs=2))
-        summed = ctx.enter_context(tc.tile_pool(name="summed", bufs=3))
+        summed = ctx.enter_context(tc.tile_pool(name="summed", bufs=2))
         regrouped = ctx.enter_context(tc.tile_pool(name="regrouped", bufs=2))
-        quantised = ctx.enter_context(tc.tile_pool(name="quantised", bufs=LEAD + 2))
-        weights = ctx.enter_context(tc.tile_pool(name="weights", bufs=3))
-        flipped = ctx.enter_context(tc.psum_pool(name="flipped", bufs=4))
+        own_quantised = ctx.enter_context(tc.tile_pool(name="own_quantised", bufs=LAG + 2))
+        agg_quantised = ctx.enter_context(tc.tile_pool(name="agg_quantised", bufs=N_CHUNKS))
+        weights = ctx.enter_context(tc.tile_pool(name="weights", bufs=4))
+        flipped = ctx.enter_context(tc.psum_pool(name="flipped", bufs=6))
         product = ctx.enter_context(tc.psum_pool(name="product", bufs=1))
+        quantised = (own_quantised, agg_quantised)
 
         identity = const.tile([P, P], F32)
         make_identity(nc, identity[:])
@@ -60,127 +67,127 @@ def tile_graphsage_pa_k_kernel(
         acc = product.tile([P, H], F32)
 
         neighbour_rows = {}
-        own_rows = {}
-        sum_rows = {}
+        rows_to_flip = {}
+        grouped = {}
         codes = {}
         planes = {}
         words = {}
 
-        def load_features(c):
+        def load_neighbours(c):
             cols = slice(c * CHUNK, (c + 1) * CHUNK)
-            neighbour_t = features.tile([P, NEIGHBOURS, CHUNK], BF16, tag="neighbour")
-            nc.sync.dma_start(out=neighbour_t[:], in_=nf2_by_node[:, :, cols])
-            own_t = features.tile([P, CHUNK], BF16, tag="own")
-            nc.sync.dma_start(out=own_t[:], in_=nf1[:, cols])
-            neighbour_rows[c] = neighbour_t
-            own_rows[c] = own_t
+            first_two = neighbours.tile([P, 2, CHUNK], BF16, tag="first_two")
+            nc.sync.dma_start(out=first_two[:], in_=nf2_by_node[:, 0:2, cols])
+            last_two = neighbours.tile([P, 2, CHUNK], BF16, tag="last_two")
+            nc.sync.dma_start(out=last_two[:], in_=nf2_by_node[:, 2:4, cols])
+            neighbour_rows[c] = (first_two, last_two)
 
-        def load_weight_scales():
-            for a in range(2):
-                by_row = weight_scales[a].rearrange("g (h s) n -> s h g n", h=2)
-                for s in range(8):
-                    first = 32 * (s // 4) + s % 4
-                    nc.sync.dma_start(
-                        out=w_planes[first:P:64, a, :, :].bitcast(I32), in_=by_row[s]
-                    )
+        def load_own(c):
+            own_t = own_features.tile([P, CHUNK], BF16, tag="own")
+            nc.sync.dma_start(out=own_t[:], in_=nf1[:, c * CHUNK : (c + 1) * CHUNK])
+            rows_to_flip[(OWN, c)] = own_t
 
-        def load_weight_words(c):
-            for a in range(2):
-                words_t = weights.tile([P, CHUNK_GROUPS, 2 * H], U8, tag="words%d" % a, align_bytes=64)
+        def load_scale_rows(a, r):
+            for quadrant in (0, 2, 1, 3):
+                q = LAG * quadrant + r
+                partition = 32 * quadrant + r
                 nc.sync.dma_start(
-                    out=words_t[:].bitcast(I32),
-                    in_=weight_words[a][c * CHUNK_GROUPS : (c + 1) * CHUNK_GROUPS].rearrange(
-                        "g p n -> p g n"
-                    ),
+                    out=w_planes[partition : partition + 1, a, :, :].bitcast(I32),
+                    in_=weight_scales[a][:, q : q + 1, :].rearrange("g o n -> o g n"),
                 )
-                words[(a, c)] = words_t
 
-        def add_first_pairs(c):
-            rows = neighbour_rows[c]
-            pair01 = partial.tile([P, CHUNK], F32, tag="pair01")
-            nc.vector.tensor_tensor(out=pair01[:], in0=rows[:, 0, :], in1=rows[:, 1, :], op=ADD)
-            pair23 = partial.tile([P, CHUNK], F32, tag="pair23")
-            nc.vector.tensor_tensor(out=pair23[:], in0=rows[:, 2, :], in1=rows[:, 3, :], op=ADD)
-            return pair01, pair23
+        def load_weight_words(a, c):
+            words_t = weights.tile([P, CHUNK_GROUPS, 2 * H], U8, tag="words", align_bytes=64)
+            nc.sync.dma_start(
+                out=words_t[:].bitcast(I32),
+                in_=weight_words[a][c * CHUNK_GROUPS : (c + 1) * CHUNK_GROUPS].rearrange(
+                    "g p n -> p g n"
+                ),
+            )
+            words[(a, c)] = words_t
 
-        def add_pairs(c, pair01, pair23):
+        def sum_neighbours(c):
+            first_two, last_two = neighbour_rows[c]
+            sum01 = partial.tile([P, CHUNK], F32, tag="sum01")
+            nc.vector.tensor_tensor(out=sum01[:], in0=first_two[:, 0, :], in1=first_two[:, 1, :], op=ADD)
+            sum23 = partial.tile([P, CHUNK], F32, tag="sum23")
+            nc.vector.tensor_tensor(out=sum23[:], in0=last_two[:, 0, :], in1=last_two[:, 1, :], op=ADD)
             sum_t = summed.tile([P, CHUNK], BF16, tag="sum")
-            nc.vector.tensor_tensor(out=sum_t[:], in0=pair01[:], in1=pair23[:], op=ADD)
-            sum_rows[c] = sum_t
+            nc.vector.tensor_tensor(out=sum_t[:], in0=sum01[:], in1=sum23[:], op=ADD)
+            rows_to_flip[(AGG, c)] = sum_t
 
-        def transpose_and_regroup(c):
-            grouped = []
-            for a, rows in enumerate((own_rows[c], sum_rows[c])):
-                row_words = rows[:].bitcast(F32)
-                grouped_t = regrouped.tile([P, CHUNK], BF16, tag="grouped%d" % a, align_bytes=64)
-                for b in range(CHUNK_GROUPS // BANK_GROUPS):
-                    bank = flipped.tile([P, 2, BANK_GROUPS, P], F32, tag="bank")
-                    for g in range(BANK_GROUPS):
-                        first = (b * BANK_GROUPS + g) * WORDS
-                        for u in range(2):
-                            nc.tensor.transpose(
-                                out=bank[:, u, g, :],
-                                in_=row_words[:, first + u : first + WORDS : 2],
-                                identity=identity[:],
-                            )
-                    nodes = slice(b * BANK_GROUPS * P, (b + 1) * BANK_GROUPS * P)
-                    if a == 0:
-                        nc.scalar.copy(
-                            out=grouped_t[:].bitcast(F32).rearrange("p (c u) -> p c u", u=2)[:, nodes, :],
-                            in_=bank[:].rearrange("p u g i -> p (g i) u"),
+        def transpose_and_regroup(a, c):
+            row_words = rows_to_flip[(a, c)][:].bitcast(F32)
+            grouped_t = regrouped.tile([P, CHUNK], BF16, tag="grouped%d" % a, align_bytes=64)
+            for b in range(CHUNK_GROUPS // BANK_GROUPS):
+                bank = flipped.tile([P, 2, BANK_GROUPS, P], F32, tag="bank")
+                for g in range(BANK_GROUPS):
+                    first = (b * BANK_GROUPS + g) * WORDS
+                    for u in range(2):
+                        nc.tensor.transpose(
+                            out=bank[:, u, g, :],
+                            in_=row_words[:, first + u : first + WORDS : 2],
+                            identity=identity[:],
                         )
-                    else:
-                        nc.scalar.activation(
-                            out=grouped_t[:].rearrange("p (c u e) -> p c u e", u=2, e=2)[:, nodes, :, :],
-                            in_=bank[:].bitcast(BF16).rearrange("p u g (i e) -> p (g i) u e", e=2),
-                            func=COPY,
-                            scale=1.0 / NEIGHBOURS,
-                        )
-                grouped.append(grouped_t)
-            return grouped
-
-        def quantise(c, grouped):
-            for a in range(2):
-                codes_t = quantised.tile([P, CHUNK_GROUPS * P], U32, tag="codes%d" % a, align_bytes=64)
-                plane_t = quantised.tile([P, CHUNK_GROUPS * P], U8, tag="plane%d" % a, align_bytes=64)
-                nc.vector.quantize_mx(
-                    out=codes_t[:].bitcast(FP8X4), scales=plane_t[:], in_=grouped[a][:]
-                )
-                codes[(a, c)] = codes_t
-                planes[(a, c)] = plane_t
-
-        def multiply(c):
-            for a in range(2):
-                for g in range(CHUNK_GROUPS):
-                    nodes = slice(g * P, (g + 1) * P)
-                    nc.tensor.matmul_mx(
-                        out=acc[:],
-                        lhsT=codes[(a, c)][:, nodes].bitcast(FP8X4),
-                        lhsT_scale=planes[(a, c)][:, nodes],
-                        rhs=words[(a, c)][:, g, :].bitcast(FP4X4),
-                        rhs_scale=w_planes[:, a, c * CHUNK_GROUPS + g, :],
-                        start=(c == 0 and a == 0 and g == 0),
-                        stop=(c == N_CHUNKS - 1 and a == 1 and g == CHUNK_GROUPS - 1),
+                nodes = slice(b * BANK_GROUPS * P, (b + 1) * BANK_GROUPS * P)
+                if a == OWN:
+                    nc.scalar.copy(
+                        out=grouped_t[:].bitcast(F32).rearrange("p (c u) -> p c u", u=2)[:, nodes, :],
+                        in_=bank[:].rearrange("p u g i -> p (g i) u"),
                     )
+                else:
+                    nc.scalar.activation(
+                        out=grouped_t[:].rearrange("p (c u e) -> p c u e", u=2, e=2)[:, nodes, :, :],
+                        in_=bank[:].bitcast(BF16).rearrange("p u g (i e) -> p (g i) u e", e=2),
+                        func=COPY,
+                        scale=1.0 / NEIGHBOURS,
+                    )
+            grouped[(a, c)] = grouped_t
 
-        grouped_of = {}
-        for s in range(N_CHUNKS + LEAD):
+        def quantise(a, c):
+            codes_t = quantised[a].tile([P, CHUNK_GROUPS * P], U32, tag="codes", align_bytes=64)
+            plane_t = quantised[a].tile([P, CHUNK_GROUPS * P], U8, tag="plane", align_bytes=64)
+            nc.vector.quantize_mx(
+                out=codes_t[:].bitcast(FP8X4), scales=plane_t[:], in_=grouped[(a, c)][:]
+            )
+            codes[(a, c)] = codes_t
+            planes[(a, c)] = plane_t
+
+        def multiply(a, c):
+            for g in range(CHUNK_GROUPS):
+                nodes = slice(g * P, (g + 1) * P)
+                nc.tensor.matmul_mx(
+                    out=acc[:],
+                    lhsT=codes[(a, c)][:, nodes].bitcast(FP8X4),
+                    lhsT_scale=planes[(a, c)][:, nodes],
+                    rhs=words[(a, c)][:, g, :].bitcast(FP4X4),
+                    rhs_scale=w_planes[:, a, c * CHUNK_GROUPS + g, :],
+                    start=(a == OWN and c == 0 and g == 0),
+                    stop=(a == AGG and c == N_CHUNKS - 1 and g == CHUNK_GROUPS - 1),
+                )
+
+        load_neighbours(0)
+        sum_neighbours(0)
+        for s in range(N_CHUNKS + LAG):
+            if s + 1 < N_CHUNKS:
+                load_neighbours(s + 1)
             if s < N_CHUNKS:
-                load_features(s)
-            if s == LEAD:
-                load_weight_scales()
-            if s >= LEAD:
-                load_weight_words(s - LEAD)
+                load_own(s)
+                load_scale_rows(s // LAG, s % LAG)
+            if s >= LAG:
+                load_weight_words(OWN, s - LAG)
             if s < N_CHUNKS:
-                pair01, pair23 = add_first_pairs(s)
-            if 1 <= s <= N_CHUNKS:
-                quantise(s - 1, grouped_of[s - 1])
+                transpose_and_regroup(AGG, s)
+                transpose_and_regroup(OWN, s)
+            if s + 1 < N_CHUNKS:
+                sum_neighbours(s + 1)
             if s < N_CHUNKS:
-                add_pairs(s, pair01, pair23)
-            if s >= LEAD:
-                multiply(s - LEAD)
-            if s < N_CHUNKS:
-                grouped_of[s] = transpose_and_regroup(s)
+                quantise(AGG, s)
+                quantise(OWN, s)
+            if s >= LAG:
+                multiply(OWN, s - LAG)
+        for c in range(N_CHUNKS):
+            load_weight_words(AGG, c)
+            multiply(AGG, c)
 
         result = const.tile([P, H], F32)
         nc.scalar.activation(out=result[:], in_=acc[:], func=RELU)

@@ -30,7 +30,9 @@ OWN = 0
 AGG = 1
 SCALE_ROWS = K_PASS // 32
 QUADRANTS = 4
-LAG = SCALE_ROWS // QUADRANTS
+BATCHES = 2 * SCALE_ROWS // QUADRANTS
+AHEAD = 2
+LAG = 2
 
 FLOPS = 2 * 2 * P * D * H
 
@@ -46,17 +48,15 @@ def tile_graphsage_pa_k_kernel(
     with ExitStack() as ctx:
         ctx.enter_context(tc.manual_schedule())
         const = ctx.enter_context(tc.tile_pool(name="const", bufs=1))
-        neighbours = ctx.enter_context(tc.tile_pool(name="neighbours", bufs=4))
+        neighbours = ctx.enter_context(tc.tile_pool(name="neighbours", bufs=AHEAD + 2))
         own_features = ctx.enter_context(tc.tile_pool(name="own_features", bufs=3))
         partial = ctx.enter_context(tc.tile_pool(name="partial", bufs=2))
-        summed = ctx.enter_context(tc.tile_pool(name="summed", bufs=2))
+        summed = ctx.enter_context(tc.tile_pool(name="summed", bufs=AHEAD + 2))
         regrouped = ctx.enter_context(tc.tile_pool(name="regrouped", bufs=2))
-        own_quantised = ctx.enter_context(tc.tile_pool(name="own_quantised", bufs=LAG + 2))
-        agg_quantised = ctx.enter_context(tc.tile_pool(name="agg_quantised", bufs=N_CHUNKS))
-        weights = ctx.enter_context(tc.tile_pool(name="weights", bufs=4))
+        quantised = ctx.enter_context(tc.tile_pool(name="quantised", bufs=LAG + 2))
+        weights = ctx.enter_context(tc.tile_pool(name="weights", bufs=3))
         flipped = ctx.enter_context(tc.psum_pool(name="flipped", bufs=6))
         product = ctx.enter_context(tc.psum_pool(name="product", bufs=1))
-        quantised = (own_quantised, agg_quantised)
 
         identity = const.tile([P, P], F32)
         make_identity(nc, identity[:])
@@ -67,28 +67,34 @@ def tile_graphsage_pa_k_kernel(
         acc = product.tile([P, H], F32)
 
         neighbour_rows = {}
+        pair_sums = {}
         rows_to_flip = {}
         grouped = {}
         codes = {}
         planes = {}
         words = {}
+        batches_loaded = [0]
 
-        def load_neighbours(c):
-            cols = slice(c * CHUNK, (c + 1) * CHUNK)
-            first_two = neighbours.tile([P, 2, CHUNK], BF16, tag="first_two")
-            nc.sync.dma_start(out=first_two[:], in_=nf2_by_node[:, 0:2, cols])
-            last_two = neighbours.tile([P, 2, CHUNK], BF16, tag="last_two")
-            nc.sync.dma_start(out=last_two[:], in_=nf2_by_node[:, 2:4, cols])
-            neighbour_rows[c] = (first_two, last_two)
+        def load_neighbour_pair(c, pair):
+            two_rows = neighbours.tile([P, 2, CHUNK], BF16, tag="pair%d" % pair)
+            nc.sync.dma_start(
+                out=two_rows[:],
+                in_=nf2_by_node[:, 2 * pair : 2 * pair + 2, c * CHUNK : (c + 1) * CHUNK],
+            )
+            neighbour_rows[(c, pair)] = two_rows
 
         def load_own(c):
             own_t = own_features.tile([P, CHUNK], BF16, tag="own")
             nc.sync.dma_start(out=own_t[:], in_=nf1[:, c * CHUNK : (c + 1) * CHUNK])
             rows_to_flip[(OWN, c)] = own_t
 
-        def load_scale_rows(a, r):
+        def load_next_scale_rows():
+            if batches_loaded[0] == BATCHES:
+                return
+            a, r = divmod(batches_loaded[0], BATCHES // 2)
+            batches_loaded[0] += 1
             for quadrant in (0, 2, 1, 3):
-                q = LAG * quadrant + r
+                q = (SCALE_ROWS // QUADRANTS) * quadrant + r
                 partition = 32 * quadrant + r
                 nc.sync.dma_start(
                     out=w_planes[partition : partition + 1, a, :, :].bitcast(I32),
@@ -96,7 +102,7 @@ def tile_graphsage_pa_k_kernel(
                 )
 
         def load_weight_words(a, c):
-            words_t = weights.tile([P, CHUNK_GROUPS, 2 * H], U8, tag="words", align_bytes=64)
+            words_t = weights.tile([P, CHUNK_GROUPS, 2 * H], U8, tag="words%d" % a, align_bytes=64)
             nc.sync.dma_start(
                 out=words_t[:].bitcast(I32),
                 in_=weight_words[a][c * CHUNK_GROUPS : (c + 1) * CHUNK_GROUPS].rearrange(
@@ -105,14 +111,17 @@ def tile_graphsage_pa_k_kernel(
             )
             words[(a, c)] = words_t
 
-        def sum_neighbours(c):
-            first_two, last_two = neighbour_rows[c]
-            sum01 = partial.tile([P, CHUNK], F32, tag="sum01")
-            nc.vector.tensor_tensor(out=sum01[:], in0=first_two[:, 0, :], in1=first_two[:, 1, :], op=ADD)
-            sum23 = partial.tile([P, CHUNK], F32, tag="sum23")
-            nc.vector.tensor_tensor(out=sum23[:], in0=last_two[:, 0, :], in1=last_two[:, 1, :], op=ADD)
+        def add_neighbour_pair(c, pair):
+            two_rows = neighbour_rows[(c, pair)]
+            pair_sum = partial.tile([P, CHUNK], F32, tag="pair_sum%d" % pair)
+            nc.vector.tensor_tensor(out=pair_sum[:], in0=two_rows[:, 0, :], in1=two_rows[:, 1, :], op=ADD)
+            pair_sums[(c, pair)] = pair_sum
+
+        def add_pair_sums(c):
             sum_t = summed.tile([P, CHUNK], BF16, tag="sum")
-            nc.vector.tensor_tensor(out=sum_t[:], in0=sum01[:], in1=sum23[:], op=ADD)
+            nc.vector.tensor_tensor(
+                out=sum_t[:], in0=pair_sums[(c, 0)][:], in1=pair_sums[(c, 1)][:], op=ADD
+            )
             rows_to_flip[(AGG, c)] = sum_t
 
         def transpose_and_regroup(a, c):
@@ -144,8 +153,8 @@ def tile_graphsage_pa_k_kernel(
             grouped[(a, c)] = grouped_t
 
         def quantise(a, c):
-            codes_t = quantised[a].tile([P, CHUNK_GROUPS * P], U32, tag="codes", align_bytes=64)
-            plane_t = quantised[a].tile([P, CHUNK_GROUPS * P], U8, tag="plane", align_bytes=64)
+            codes_t = quantised.tile([P, CHUNK_GROUPS * P], U32, tag="codes%d" % a, align_bytes=64)
+            plane_t = quantised.tile([P, CHUNK_GROUPS * P], U8, tag="plane%d" % a, align_bytes=64)
             nc.vector.quantize_mx(
                 out=codes_t[:].bitcast(FP8X4), scales=plane_t[:], in_=grouped[(a, c)][:]
             )
@@ -165,29 +174,38 @@ def tile_graphsage_pa_k_kernel(
                     stop=(a == AGG and c == N_CHUNKS - 1 and g == CHUNK_GROUPS - 1),
                 )
 
-        load_neighbours(0)
-        sum_neighbours(0)
+        for c in range(AHEAD):
+            for pair in range(2):
+                load_neighbour_pair(c, pair)
+                if (c, pair) != (0, 0):
+                    load_next_scale_rows()
+                add_neighbour_pair(c, pair)
+            add_pair_sums(c)
         for s in range(N_CHUNKS + LAG):
-            if s + 1 < N_CHUNKS:
-                load_neighbours(s + 1)
+            early = s + AHEAD
+            late = s - LAG
+            if early < N_CHUNKS:
+                for pair in range(2):
+                    load_neighbour_pair(early, pair)
+                    load_next_scale_rows()
+                    add_neighbour_pair(early, pair)
             if s < N_CHUNKS:
                 load_own(s)
-                load_scale_rows(s // LAG, s % LAG)
-            if s >= LAG:
-                load_weight_words(OWN, s - LAG)
+                load_next_scale_rows()
+            if late >= 0:
+                load_weight_words(OWN, late)
+                load_weight_words(AGG, late)
             if s < N_CHUNKS:
                 transpose_and_regroup(AGG, s)
                 transpose_and_regroup(OWN, s)
-            if s + 1 < N_CHUNKS:
-                sum_neighbours(s + 1)
-            if s < N_CHUNKS:
                 quantise(AGG, s)
+            if early < N_CHUNKS:
+                add_pair_sums(early)
+            if s < N_CHUNKS:
                 quantise(OWN, s)
-            if s >= LAG:
-                multiply(OWN, s - LAG)
-        for c in range(N_CHUNKS):
-            load_weight_words(AGG, c)
-            multiply(AGG, c)
+            if late >= 0:
+                multiply(OWN, late)
+                multiply(AGG, late)
 
         result = const.tile([P, H], F32)
         nc.scalar.activation(out=result[:], in_=acc[:], func=RELU)

@@ -61,8 +61,11 @@ def tile_graphsage_pa_k_kernel(
         identity = const.tile([P, P], F32)
         make_identity(nc, identity[:])
 
-        w_planes = const.tile([P, 2, GROUPS, H], U8, align_bytes=64)
-        nc.vector.memset(w_planes[:].bitcast(I32), 0)
+        own_planes = const.tile([P, GROUPS, H], U8, align_bytes=64)
+        agg_planes = const.tile([P, GROUPS, H], U8, align_bytes=64)
+        w_planes = (own_planes, agg_planes)
+        nc.vector.memset(own_planes[:].bitcast(I32), 0)
+        nc.gpsimd.memset(agg_planes[:].bitcast(I32), 0)
 
         acc = product.tile([P, H], F32)
 
@@ -97,7 +100,7 @@ def tile_graphsage_pa_k_kernel(
                 q = (SCALE_ROWS // QUADRANTS) * quadrant + r
                 partition = 32 * quadrant + r
                 nc.sync.dma_start(
-                    out=w_planes[partition : partition + 1, a, :, :].bitcast(I32),
+                    out=w_planes[a][partition : partition + 1, :, :].bitcast(I32),
                     in_=weight_scales[a][:, q : q + 1, :].rearrange("g o n -> o g n"),
                 )
 
@@ -169,7 +172,7 @@ def tile_graphsage_pa_k_kernel(
                     lhsT=codes[(a, c)][:, nodes].bitcast(FP8X4),
                     lhsT_scale=planes[(a, c)][:, nodes],
                     rhs=words[(a, c)][:, g, :].bitcast(FP4X4),
-                    rhs_scale=w_planes[:, a, c * CHUNK_GROUPS + g, :],
+                    rhs_scale=w_planes[a][:, c * CHUNK_GROUPS + g, :],
                     start=(a == OWN and c == 0 and g == 0),
                     stop=(a == AGG and c == N_CHUNKS - 1 and g == CHUNK_GROUPS - 1),
                 )

@@ -11,6 +11,7 @@ U8 = mybir.dt.uint8
 FP8X4 = mybir.dt.float8_e4m3fn_x4
 FP4X4 = mybir.dt.float4_e2m1fn_x4
 ADD = mybir.AluOpType.add
+MULT = mybir.AluOpType.mult
 COPY = mybir.ActivationFunctionType.Copy
 RELU = mybir.ActivationFunctionType.Relu
 
@@ -32,6 +33,9 @@ SCALE_ROWS = K_PASS // 32
 QUADRANTS = 4
 BATCHES = 2 * SCALE_ROWS // QUADRANTS
 AHEAD = 2
+VECTOR_CHUNKS = 2
+BLOCKS = NEIGHBOURS
+BLOCK_NODES = P // NEIGHBOURS
 LAG = 2
 
 FLOPS = 2 * 2 * P * D * H
@@ -44,6 +48,7 @@ def tile_graphsage_pa_k_kernel(
     weight_words = (w2_0_words.bitcast(I32), w1_0_words.bitcast(I32))
     weight_scales = (w2_0_scales.bitcast(I32), w1_0_scales.bitcast(I32))
     nf2_by_node = nf2.rearrange("(i j) d -> i j d", j=NEIGHBOURS)
+    nf2_by_block = nf2.rearrange("(b r) d -> r b d", r=P)
 
     with ExitStack() as ctx:
         ctx.enter_context(tc.manual_schedule())
@@ -61,11 +66,23 @@ def tile_graphsage_pa_k_kernel(
         identity = const.tile([P, P], F32)
         make_identity(nc, identity[:])
 
+        ones = const.tile([P, BLOCK_NODES], F32)
+        pooling = const.tile([P, BLOCK_NODES], BF16)
+
         own_planes = const.tile([P, GROUPS, H], U8, align_bytes=64)
         agg_planes = const.tile([P, GROUPS, H], U8, align_bytes=64)
         w_planes = (own_planes, agg_planes)
         nc.vector.memset(own_planes[:].bitcast(I32), 0)
         nc.gpsimd.memset(agg_planes[:].bitcast(I32), 0)
+        nc.vector.tensor_reduce(
+            out=ones[:],
+            in_=identity[:].rearrange("r (i j) -> r i j", j=NEIGHBOURS),
+            axis=mybir.AxisListType.X,
+            op=ADD,
+        )
+        nc.vector.tensor_scalar(
+            out=pooling[:], in0=ones[:], scalar1=1.0 / NEIGHBOURS, scalar2=None, op0=MULT
+        )
 
         acc = product.tile([P, H], F32)
 
@@ -80,9 +97,10 @@ def tile_graphsage_pa_k_kernel(
 
         def load_neighbour_pair(c, pair):
             two_rows = neighbours.tile([P, 2, CHUNK], BF16, tag="pair%d" % pair)
+            view = nf2_by_node if c < VECTOR_CHUNKS else nf2_by_block
             nc.sync.dma_start(
                 out=two_rows[:],
-                in_=nf2_by_node[:, 2 * pair : 2 * pair + 2, c * CHUNK : (c + 1) * CHUNK],
+                in_=view[:, 2 * pair : 2 * pair + 2, c * CHUNK : (c + 1) * CHUNK],
             )
             neighbour_rows[(c, pair)] = two_rows
 
@@ -155,6 +173,26 @@ def tile_graphsage_pa_k_kernel(
                     )
             grouped[(a, c)] = grouped_t
 
+        def pool_and_regroup(c):
+            grouped_t = regrouped.tile([P, CHUNK], BF16, tag="grouped%d" % AGG, align_bytes=64)
+            for g in range(CHUNK_GROUPS):
+                bank = flipped.tile([P, PACK, P], F32, tag="bank")
+                for b in range(BLOCKS):
+                    rows = neighbour_rows[(c, b // 2)]
+                    for t in range(PACK):
+                        nc.tensor.matmul(
+                            out=bank[:, t, b * BLOCK_NODES : (b + 1) * BLOCK_NODES],
+                            lhsT=rows[:, b % 2, g * K_PASS + t : (g + 1) * K_PASS : PACK],
+                            rhs=pooling[:],
+                            start=True,
+                            stop=True,
+                        )
+                nc.scalar.copy(
+                    out=grouped_t[:, g * K_PASS : (g + 1) * K_PASS].rearrange("p (i t) -> p i t", t=PACK),
+                    in_=bank[:].rearrange("p t i -> p i t"),
+                )
+            grouped[(AGG, c)] = grouped_t
+
         def quantise(a, c):
             codes_t = quantised.tile([P, CHUNK_GROUPS * P], U32, tag="codes%d" % a, align_bytes=64)
             plane_t = quantised.tile([P, CHUNK_GROUPS * P], U8, tag="plane%d" % a, align_bytes=64)
@@ -191,7 +229,6 @@ def tile_graphsage_pa_k_kernel(
                 for pair in range(2):
                     load_neighbour_pair(early, pair)
                     load_next_scale_rows()
-                    add_neighbour_pair(early, pair)
             if s < N_CHUNKS:
                 load_own(s)
                 load_next_scale_rows()
@@ -199,12 +236,12 @@ def tile_graphsage_pa_k_kernel(
                 load_weight_words(OWN, late)
                 load_weight_words(AGG, late)
             if s < N_CHUNKS:
-                transpose_and_regroup(AGG, s)
+                if s < VECTOR_CHUNKS:
+                    transpose_and_regroup(AGG, s)
+                else:
+                    pool_and_regroup(s)
                 transpose_and_regroup(OWN, s)
                 quantise(AGG, s)
-            if early < N_CHUNKS:
-                add_pair_sums(early)
-            if s < N_CHUNKS:
                 quantise(OWN, s)
             if late >= 0:
                 multiply(OWN, late)

@@ -33,7 +33,7 @@ SCALE_ROWS = K_PASS // 32
 QUADRANTS = 4
 BATCHES = 2 * SCALE_ROWS // QUADRANTS
 AHEAD = 2
-VECTOR_CHUNKS = 2
+POOL_EVERY = 3
 BLOCKS = NEIGHBOURS
 BLOCK_NODES = P // NEIGHBOURS
 LAG = 2
@@ -95,9 +95,12 @@ def tile_graphsage_pa_k_kernel(
         words = {}
         batches_loaded = [0]
 
+        def pooled_on_tensor(c):
+            return c % POOL_EVERY == POOL_EVERY - 1
+
         def load_neighbour_pair(c, pair):
             two_rows = neighbours.tile([P, 2, CHUNK], BF16, tag="pair%d" % pair)
-            view = nf2_by_node if c < VECTOR_CHUNKS else nf2_by_block
+            view = nf2_by_block if pooled_on_tensor(c) else nf2_by_node
             nc.sync.dma_start(
                 out=two_rows[:],
                 in_=view[:, 2 * pair : 2 * pair + 2, c * CHUNK : (c + 1) * CHUNK],
@@ -229,6 +232,8 @@ def tile_graphsage_pa_k_kernel(
                 for pair in range(2):
                     load_neighbour_pair(early, pair)
                     load_next_scale_rows()
+                    if not pooled_on_tensor(early):
+                        add_neighbour_pair(early, pair)
             if s < N_CHUNKS:
                 load_own(s)
                 load_next_scale_rows()
@@ -236,12 +241,15 @@ def tile_graphsage_pa_k_kernel(
                 load_weight_words(OWN, late)
                 load_weight_words(AGG, late)
             if s < N_CHUNKS:
-                if s < VECTOR_CHUNKS:
-                    transpose_and_regroup(AGG, s)
-                else:
+                if pooled_on_tensor(s):
                     pool_and_regroup(s)
+                else:
+                    transpose_and_regroup(AGG, s)
                 transpose_and_regroup(OWN, s)
                 quantise(AGG, s)
+            if early < N_CHUNKS and not pooled_on_tensor(early):
+                add_pair_sums(early)
+            if s < N_CHUNKS:
                 quantise(OWN, s)
             if late >= 0:
                 multiply(OWN, late)

@@ -31,12 +31,12 @@ OWN = 0
 AGG = 1
 SCALE_ROWS = K_PASS // 32
 QUADRANTS = 4
-BATCHES = 2 * SCALE_ROWS // QUADRANTS
-AHEAD = 2
+SCALE_DMAS = 2
+AHEAD = 1
 POOL_EVERY = 3
 BLOCKS = NEIGHBOURS
 BLOCK_NODES = P // NEIGHBOURS
-LAG = 2
+LAG = 4
 
 FLOPS = 2 * 2 * P * D * H
 
@@ -53,7 +53,7 @@ def tile_graphsage_pa_k_kernel(
     with ExitStack() as ctx:
         ctx.enter_context(tc.manual_schedule())
         const = ctx.enter_context(tc.tile_pool(name="const", bufs=1))
-        neighbours = ctx.enter_context(tc.tile_pool(name="neighbours", bufs=AHEAD + 2))
+        neighbours = ctx.enter_context(tc.tile_pool(name="neighbours", bufs=AHEAD + 3))
         own_features = ctx.enter_context(tc.tile_pool(name="own_features", bufs=3))
         partial = ctx.enter_context(tc.tile_pool(name="partial", bufs=2))
         summed = ctx.enter_context(tc.tile_pool(name="summed", bufs=AHEAD + 2))
@@ -93,7 +93,7 @@ def tile_graphsage_pa_k_kernel(
         codes = {}
         planes = {}
         words = {}
-        batches_loaded = [0]
+        rows_loaded = [0]
 
         def pooled_on_tensor(c):
             return c % POOL_EVERY == POOL_EVERY - 1
@@ -113,17 +113,17 @@ def tile_graphsage_pa_k_kernel(
             rows_to_flip[(OWN, c)] = own_t
 
         def load_next_scale_rows():
-            if batches_loaded[0] == BATCHES:
-                return
-            a, r = divmod(batches_loaded[0], BATCHES // 2)
-            batches_loaded[0] += 1
-            for quadrant in (0, 2, 1, 3):
+            for i in range(rows_loaded[0], min(rows_loaded[0] + SCALE_DMAS, 2 * SCALE_ROWS)):
+                a, row = divmod(i, SCALE_ROWS)
+                r, turn = divmod(row, QUADRANTS)
+                quadrant = (0, 2, 1, 3)[turn]
                 q = (SCALE_ROWS // QUADRANTS) * quadrant + r
                 partition = 32 * quadrant + r
                 nc.sync.dma_start(
                     out=w_planes[a][partition : partition + 1, :, :].bitcast(I32),
                     in_=weight_scales[a][:, q : q + 1, :].rearrange("g o n -> o g n"),
                 )
+            rows_loaded[0] += SCALE_DMAS
 
         def load_weight_words(a, c):
             words_t = weights.tile([P, CHUNK_GROUPS, 2 * H], U8, tag="words%d" % a, align_bytes=64)

@@ -37,6 +37,7 @@ POOL_EVERY = 3
 BLOCKS = NEIGHBOURS
 BLOCK_NODES = P // NEIGHBOURS
 LAG = 4
+LAST_PIECES = ((2, 2), (2, 1, 1))
 
 FLOPS = 2 * 2 * P * D * H
 
@@ -55,11 +56,11 @@ def tile_graphsage_pa_k_kernel(
         const = ctx.enter_context(tc.tile_pool(name="const", bufs=1))
         neighbours = ctx.enter_context(tc.tile_pool(name="neighbours", bufs=AHEAD + 3))
         own_features = ctx.enter_context(tc.tile_pool(name="own_features", bufs=3))
-        partial = ctx.enter_context(tc.tile_pool(name="partial", bufs=2))
+        partial = ctx.enter_context(tc.tile_pool(name="partial", bufs=1))
         summed = ctx.enter_context(tc.tile_pool(name="summed", bufs=AHEAD + 2))
         regrouped = ctx.enter_context(tc.tile_pool(name="regrouped", bufs=2))
         quantised = ctx.enter_context(tc.tile_pool(name="quantised", bufs=LAG + 2))
-        weights = ctx.enter_context(tc.tile_pool(name="weights", bufs=3))
+        weights = ctx.enter_context(tc.tile_pool(name="weights", bufs=5))
         flipped = ctx.enter_context(tc.psum_pool(name="flipped", bufs=6))
         product = ctx.enter_context(tc.psum_pool(name="product", bufs=1))
 
@@ -127,12 +128,14 @@ def tile_graphsage_pa_k_kernel(
 
         def load_weight_words(a, c):
             words_t = weights.tile([P, CHUNK_GROUPS, 2 * H], U8, tag="words%d" % a, align_bytes=64)
-            nc.sync.dma_start(
-                out=words_t[:].bitcast(I32),
-                in_=weight_words[a][c * CHUNK_GROUPS : (c + 1) * CHUNK_GROUPS].rearrange(
-                    "g p n -> p g n"
-                ),
-            )
+            first = 0
+            for count in LAST_PIECES[a] if c == N_CHUNKS - 1 else (CHUNK_GROUPS,):
+                g = c * CHUNK_GROUPS + first
+                nc.sync.dma_start(
+                    out=words_t[:, first : first + count, :].bitcast(I32),
+                    in_=weight_words[a][g : g + count].rearrange("g p n -> p g n"),
+                )
+                first += count
             words[(a, c)] = words_t
 
         def add_neighbour_pair(c, pair):
@@ -240,7 +243,13 @@ def tile_graphsage_pa_k_kernel(
             if late >= 0:
                 load_weight_words(OWN, late)
                 load_weight_words(AGG, late)
-            if s < N_CHUNKS:
+            if s == N_CHUNKS - 1:
+                transpose_and_regroup(OWN, s)
+                multiply(OWN, late)
+                multiply(AGG, late)
+                transpose_and_regroup(AGG, s)
+                quantise(AGG, s)
+            elif s < N_CHUNKS:
                 if pooled_on_tensor(s):
                     pool_and_regroup(s)
                 else:
@@ -251,7 +260,7 @@ def tile_graphsage_pa_k_kernel(
                 add_pair_sums(early)
             if s < N_CHUNKS:
                 quantise(OWN, s)
-            if late >= 0:
+            if late >= 0 and s != N_CHUNKS - 1:
                 multiply(OWN, late)
                 multiply(AGG, late)
 

from contextlib import ExitStack

import concourse.mybir as mybir
from concourse.masks import make_identity

F32 = mybir.dt.float32
BF16 = mybir.dt.bfloat16
I32 = mybir.dt.int32
U32 = mybir.dt.uint32
U8 = mybir.dt.uint8
FP8X4 = mybir.dt.float8_e4m3fn_x4
FP4X4 = mybir.dt.float4_e2m1fn_x4
ADD = mybir.AluOpType.add
MULT = mybir.AluOpType.mult
COPY = mybir.ActivationFunctionType.Copy
RELU = mybir.ActivationFunctionType.Relu

P = 128
NEIGHBOURS = 4
D = 16384
H = 512
PACK = 4
K_PASS = P * PACK
GROUPS = D // K_PASS
CHUNK_GROUPS = 4
CHUNK = CHUNK_GROUPS * K_PASS
N_CHUNKS = GROUPS // CHUNK_GROUPS
BANK_GROUPS = 2
WORDS = K_PASS // 2
OWN = 0
AGG = 1
SCALE_ROWS = K_PASS // 32
QUADRANTS = 4
SCALE_DMAS = 2
AHEAD = 1
POOL_EVERY = 3
BLOCKS = NEIGHBOURS
BLOCK_NODES = P // NEIGHBOURS
LAG = 4
LAST_PIECES = ((2, 2), (2, 1, 1))

FLOPS = 2 * 2 * P * D * H


def tile_graphsage_pa_k_kernel(
    tc, nf1, nf2, w1_0_words, w1_0_scales, w2_0_words, w2_0_scales, out
):
    nc = tc.nc
    weight_words = (w2_0_words.bitcast(I32), w1_0_words.bitcast(I32))
    weight_scales = (w2_0_scales.bitcast(I32), w1_0_scales.bitcast(I32))
    nf2_by_node = nf2.rearrange("(i j) d -> i j d", j=NEIGHBOURS)
    nf2_by_block = nf2.rearrange("(b r) d -> r b d", r=P)

    with ExitStack() as ctx:
        ctx.enter_context(tc.manual_schedule())
        const = ctx.enter_context(tc.tile_pool(name="const", bufs=1))
        neighbours = ctx.enter_context(tc.tile_pool(name="neighbours", bufs=AHEAD + 3))
        own_features = ctx.enter_context(tc.tile_pool(name="own_features", bufs=3))
        partial = ctx.enter_context(tc.tile_pool(name="partial", bufs=1))
        summed = ctx.enter_context(tc.tile_pool(name="summed", bufs=AHEAD + 2))
        regrouped = ctx.enter_context(tc.tile_pool(name="regrouped", bufs=2))
        quantised = ctx.enter_context(tc.tile_pool(name="quantised", bufs=LAG + 2))
        weights = ctx.enter_context(tc.tile_pool(name="weights", bufs=5))
        flipped = ctx.enter_context(tc.psum_pool(name="flipped", bufs=6))
        product = ctx.enter_context(tc.psum_pool(name="product", bufs=1))

        identity = const.tile([P, P], F32)
        make_identity(nc, identity[:])

        ones = const.tile([P, BLOCK_NODES], F32)
        pooling = const.tile([P, BLOCK_NODES], BF16)

        own_planes = const.tile([P, GROUPS, H], U8, align_bytes=64)
        agg_planes = const.tile([P, GROUPS, H], U8, align_bytes=64)
        w_planes = (own_planes, agg_planes)
        nc.vector.memset(own_planes[:].bitcast(I32), 0)
        nc.gpsimd.memset(agg_planes[:].bitcast(I32), 0)
        nc.vector.tensor_reduce(
            out=ones[:],
            in_=identity[:].rearrange("r (i j) -> r i j", j=NEIGHBOURS),
            axis=mybir.AxisListType.X,
            op=ADD,
        )
        nc.vector.tensor_scalar(
            out=pooling[:], in0=ones[:], scalar1=1.0 / NEIGHBOURS, scalar2=None, op0=MULT
        )

        acc = product.tile([P, H], F32)

        neighbour_rows = {}
        pair_sums = {}
        rows_to_flip = {}
        grouped = {}
        codes = {}
        planes = {}
        words = {}
        rows_loaded = [0]

        def pooled_on_tensor(c):
            return c % POOL_EVERY == POOL_EVERY - 1

        def load_neighbour_pair(c, pair):
            two_rows = neighbours.tile([P, 2, CHUNK], BF16, tag="pair%d" % pair)
            view = nf2_by_block if pooled_on_tensor(c) else nf2_by_node
            nc.sync.dma_start(
                out=two_rows[:],
                in_=view[:, 2 * pair : 2 * pair + 2, c * CHUNK : (c + 1) * CHUNK],
            )
            neighbour_rows[(c, pair)] = two_rows

        def load_own(c):
            own_t = own_features.tile([P, CHUNK], BF16, tag="own")
            nc.sync.dma_start(out=own_t[:], in_=nf1[:, c * CHUNK : (c + 1) * CHUNK])
            rows_to_flip[(OWN, c)] = own_t

        def load_next_scale_rows():
            for i in range(rows_loaded[0], min(rows_loaded[0] + SCALE_DMAS, 2 * SCALE_ROWS)):
                a, row = divmod(i, SCALE_ROWS)
                r, turn = divmod(row, QUADRANTS)
                quadrant = (0, 2, 1, 3)[turn]
                q = (SCALE_ROWS // QUADRANTS) * quadrant + r
                partition = 32 * quadrant + r
                nc.sync.dma_start(
                    out=w_planes[a][partition : partition + 1, :, :].bitcast(I32),
                    in_=weight_scales[a][:, q : q + 1, :].rearrange("g o n -> o g n"),
                )
            rows_loaded[0] += SCALE_DMAS

        def load_weight_words(a, c):
            words_t = weights.tile([P, CHUNK_GROUPS, 2 * H], U8, tag="words%d" % a, align_bytes=64)
            first = 0
            for count in LAST_PIECES[a] if c == N_CHUNKS - 1 else (CHUNK_GROUPS,):
                g = c * CHUNK_GROUPS + first
                nc.sync.dma_start(
                    out=words_t[:, first : first + count, :].bitcast(I32),
                    in_=weight_words[a][g : g + count].rearrange("g p n -> p g n"),
                )
                first += count
            words[(a, c)] = words_t

        def add_neighbour_pair(c, pair):
            two_rows = neighbour_rows[(c, pair)]
            pair_sum = partial.tile([P, CHUNK], F32, tag="pair_sum%d" % pair)
            nc.vector.tensor_tensor(out=pair_sum[:], in0=two_rows[:, 0, :], in1=two_rows[:, 1, :], op=ADD)
            pair_sums[(c, pair)] = pair_sum

        def add_pair_sums(c):
            sum_t = summed.tile([P, CHUNK], BF16, tag="sum")
            nc.vector.tensor_tensor(
                out=sum_t[:], in0=pair_sums[(c, 0)][:], in1=pair_sums[(c, 1)][:], op=ADD
            )
            rows_to_flip[(AGG, c)] = sum_t

        def transpose_and_regroup(a, c):
            row_words = rows_to_flip[(a, c)][:].bitcast(F32)
            grouped_t = regrouped.tile([P, CHUNK], BF16, tag="grouped%d" % a, align_bytes=64)
            for b in range(CHUNK_GROUPS // BANK_GROUPS):
                bank = flipped.tile([P, 2, BANK_GROUPS, P], F32, tag="bank")
                for g in range(BANK_GROUPS):
                    first = (b * BANK_GROUPS + g) * WORDS
                    for u in range(2):
                        nc.tensor.transpose(
                            out=bank[:, u, g, :],
                            in_=row_words[:, first + u : first + WORDS : 2],
                            identity=identity[:],
                        )
                nodes = slice(b * BANK_GROUPS * P, (b + 1) * BANK_GROUPS * P)
                if a == OWN:
                    nc.scalar.copy(
                        out=grouped_t[:].bitcast(F32).rearrange("p (c u) -> p c u", u=2)[:, nodes, :],
                        in_=bank[:].rearrange("p u g i -> p (g i) u"),
                    )
                else:
                    nc.scalar.activation(
                        out=grouped_t[:].rearrange("p (c u e) -> p c u e", u=2, e=2)[:, nodes, :, :],
                        in_=bank[:].bitcast(BF16).rearrange("p u g (i e) -> p (g i) u e", e=2),
                        func=COPY,
                        scale=1.0 / NEIGHBOURS,
                    )
            grouped[(a, c)] = grouped_t

        def pool_and_regroup(c):
            grouped_t = regrouped.tile([P, CHUNK], BF16, tag="grouped%d" % AGG, align_bytes=64)
            for g in range(CHUNK_GROUPS):
                bank = flipped.tile([P, PACK, P], F32, tag="bank")
                for b in range(BLOCKS):
                    rows = neighbour_rows[(c, b // 2)]
                    for t in range(PACK):
                        nc.tensor.matmul(
                            out=bank[:, t, b * BLOCK_NODES : (b + 1) * BLOCK_NODES],
                            lhsT=rows[:, b % 2, g * K_PASS + t : (g + 1) * K_PASS : PACK],
                            rhs=pooling[:],
                            start=True,
                            stop=True,
                        )
                nc.scalar.copy(
                    out=grouped_t[:, g * K_PASS : (g + 1) * K_PASS].rearrange("p (i t) -> p i t", t=PACK),
                    in_=bank[:].rearrange("p t i -> p i t"),
                )
            grouped[(AGG, c)] = grouped_t

        def quantise(a, c):
            codes_t = quantised.tile([P, CHUNK_GROUPS * P], U32, tag="codes%d" % a, align_bytes=64)
            plane_t = quantised.tile([P, CHUNK_GROUPS * P], U8, tag="plane%d" % a, align_bytes=64)
            nc.vector.quantize_mx(
                out=codes_t[:].bitcast(FP8X4), scales=plane_t[:], in_=grouped[(a, c)][:]
            )
            codes[(a, c)] = codes_t
            planes[(a, c)] = plane_t

        def multiply(a, c):
            for g in range(CHUNK_GROUPS):
                nodes = slice(g * P, (g + 1) * P)
                nc.tensor.matmul_mx(
                    out=acc[:],
                    lhsT=codes[(a, c)][:, nodes].bitcast(FP8X4),
                    lhsT_scale=planes[(a, c)][:, nodes],
                    rhs=words[(a, c)][:, g, :].bitcast(FP4X4),
                    rhs_scale=w_planes[a][:, c * CHUNK_GROUPS + g, :],
                    start=(a == OWN and c == 0 and g == 0),
                    stop=(a == AGG and c == N_CHUNKS - 1 and g == CHUNK_GROUPS - 1),
                )

        for c in range(AHEAD):
            for pair in range(2):
                load_neighbour_pair(c, pair)
                if (c, pair) != (0, 0):
                    load_next_scale_rows()
                add_neighbour_pair(c, pair)
            add_pair_sums(c)
        for s in range(N_CHUNKS + LAG):
            early = s + AHEAD
            late = s - LAG
            if early < N_CHUNKS:
                for pair in range(2):
                    load_neighbour_pair(early, pair)
                    load_next_scale_rows()
                    if not pooled_on_tensor(early):
                        add_neighbour_pair(early, pair)
            if s < N_CHUNKS:
                load_own(s)
                load_next_scale_rows()
            if late >= 0:
                load_weight_words(OWN, late)
                load_weight_words(AGG, late)
            if s == N_CHUNKS - 1:
                transpose_and_regroup(OWN, s)
                multiply(OWN, late)
                multiply(AGG, late)
                transpose_and_regroup(AGG, s)
                quantise(AGG, s)
            elif s < N_CHUNKS:
                if pooled_on_tensor(s):
                    pool_and_regroup(s)
                else:
                    transpose_and_regroup(AGG, s)
                transpose_and_regroup(OWN, s)
                quantise(AGG, s)
            if early < N_CHUNKS and not pooled_on_tensor(early):
                add_pair_sums(early)
            if s < N_CHUNKS:
                quantise(OWN, s)
            if late >= 0 and s != N_CHUNKS - 1:
                multiply(OWN, late)
                multiply(AGG, late)

        result = const.tile([P, H], F32)
        nc.scalar.activation(out=result[:], in_=acc[:], func=RELU)
        nc.sync.dma_start(out=out, in_=result[:])
